import numpy as np
import ml_dtypes


def mxq(x, axis, fmt="e4m3"):
    dtype, down = {"e4m3": (ml_dtypes.float8_e4m3fn, 7), "e5m2": (ml_dtypes.float8_e5m2, 14)}[fmt]
    v = np.moveaxis(np.asarray(x, np.float32).astype(ml_dtypes.bfloat16).astype(np.float64), axis, -1)
    blocks = v.reshape(v.shape[:-1] + (-1, 32))
    amax = np.abs(blocks).max(-1, keepdims=True)
    byte = np.maximum(np.where(amax > 0, np.frexp(amax)[1] - 1 + 127, 0) - down, 1)
    scale = np.exp2(byte - 127.0)
    codes = (blocks / scale).astype(np.float32).astype(dtype).astype(np.float64)
    return np.moveaxis((codes * scale).reshape(v.shape), -1, axis)


WIDE = False


def mx_kscale(k):
    if not WIDE:
        return np.ones(k)
    levels = np.array([10, -10, 5, -5, 0])
    a = np.random.permutation(np.resize(levels, k // 512 * 4)).reshape(k // 512, 4)
    idx = np.arange(k)
    return np.exp2(a[idx // 512, idx % 128 // 32])


BF16 = ml_dtypes.bfloat16


def bf(x):
    return np.asarray(x, np.float32).astype(BF16)


def f64(x):
    return np.asarray(x).astype(np.float64)


B, S, HID, H, HK, D = 2, 256, 2048, 16, 4, 128
EPS = 1e-6
PRE = 0.004


def rmsnorm(v, w):
    var = np.mean(v * v, axis=-1, keepdims=True)
    return w * (v * (1.0 / np.sqrt(var + EPS)))


def rope(v, cos, sin):
    c = cos[:, :, None, :]
    sn = sin[:, :, None, :]
    v1, v2 = np.split(v, 2, axis=-1)
    rot = np.concatenate([-v2, v1], axis=-1)
    return v * c + rot * sn


def setup_inputs():
    s = mx_kscale(HID)
    return {
        "hidden_states": bf(np.random.standard_normal((B, S, HID)) * s),
        "cos": bf(np.cos(np.random.standard_normal((B, S, D)))),
        "sin": bf(np.sin(np.random.standard_normal((B, S, D)))),
        "Wq_query": bf(np.random.standard_normal((H * D, HID)) * PRE / np.sqrt(HID) / s),
        "Wk": bf(np.random.standard_normal((HK * D, HID)) * PRE / np.sqrt(HID) / s),
        "q_norm_w": bf(1.0 + 0.1 * np.random.standard_normal(D)),
        "k_norm_w": bf(1.0 + 0.1 * np.random.standard_normal(D)),
    }


def reference(hidden_states, cos, sin, Wq_query, Wk, q_norm_w, k_norm_w):
    xq = mxq(f64(hidden_states), 2, "e4m3")
    q = (xq @ mxq(f64(Wq_query), 1, "e4m3").T).reshape(B, S, H, D)
    k = (xq @ mxq(f64(Wk), 1, "e4m3").T).reshape(B, S, HK, D)
    q = rmsnorm(q, f64(q_norm_w))
    k = rmsnorm(k, f64(k_norm_w))
    q = rope(q, f64(cos), f64(sin))
    k = rope(k, f64(cos), f64(sin))
    return q, k

@@ -1,0 +1,209 @@
+from contextlib import ExitStack
+
+import concourse.mybir as mybir
+from concourse.masks import make_identity
+
+F32 = mybir.dt.float32
+BF16 = mybir.dt.bfloat16
+U32 = mybir.dt.uint32
+U8 = mybir.dt.uint8
+FP8X4 = mybir.dt.float8_e4m3fn_x4
+ACT = mybir.ActivationFunctionType
+ALU = mybir.AluOpType
+
+P = 128
+PACK = 4
+HIDDEN = 2048
+PASSES = HIDDEN // (P * PACK)
+WORDS = HIDDEN // 2
+BLOCK = 512
+HALF = BLOCK // 2
+PAIRS = 4
+HEAD = 128
+HEADS = BLOCK // HEAD
+TOKEN_TILES = 4
+Q_BLOCKS = 4
+W_BLOCKS = Q_BLOCKS + 1
+EPS = 1e-6
+
+FLOPS = 2 * 512 * (2048 + 512) * HIDDEN
+
+
+def tile_qwen3nextattentionforengine_pa_kernel(
+    tc, hidden_states, cos, sin, Wq_query, Wk, q_norm_w, k_norm_w, out_0, out_1
+):
+    nc = tc.nc
+    tokens = hidden_states.rearrange("b s k -> (b s) k")
+    q_flat = out_0.rearrange("b s h d -> (b s) (h d)")
+    k_flat = out_1.rearrange("b s h d -> (b s) (h d)")
+
+    row_blocks = [tokens] + [Wq_query[BLOCK * b : BLOCK * (b + 1), :] for b in range(Q_BLOCKS)] + [Wk]
+    results = [None] + [(q_flat[:, BLOCK * b : BLOCK * (b + 1)], 0) for b in range(Q_BLOCKS)] + [(k_flat, 1)]
+
+    with ExitStack() as ctx:
+        consts = ctx.enter_context(tc.tile_pool(name="consts", bufs=1))
+        raw_pool = ctx.enter_context(tc.tile_pool(name="raw", bufs=2 * len(row_blocks)))
+        group_pool = ctx.enter_context(tc.tile_pool(name="grouped", bufs=6))
+        weight_pool = ctx.enter_context(tc.tile_pool(name="weights", bufs=2))
+        small_pool = ctx.enter_context(tc.tile_pool(name="small", bufs=4))
+        prod_pool = ctx.enter_context(tc.tile_pool(name="prod", bufs=4))
+        result_pool = ctx.enter_context(tc.tile_pool(name="result", bufs=W_BLOCKS * TOKEN_TILES))
+        turn_psum = ctx.enter_context(tc.psum_pool(name="turn", bufs=4))
+        acc_psum = ctx.enter_context(tc.psum_pool(name="acc", bufs=4))
+
+        raws = []
+        for rows in row_blocks:
+            halves = []
+            for half in range(2):
+                raw = raw_pool.tile([P, 2 * HIDDEN], BF16, name="raw")
+                nc.sync.dma_start(
+                    out=raw[:],
+                    in_=rows[HALF * half : HALF * (half + 1), :].rearrange("(p r) k -> p (r k)", r=2),
+                )
+                halves.append(raw)
+            raws.append(halves)
+
+        cos_sb = consts.tile([P, TOKEN_TILES, HEAD], BF16, name="cos_sb")
+        sin_sb = consts.tile([P, TOKEN_TILES, HEAD], BF16, name="sin_sb")
+        gains = consts.tile([P, 2, HEAD], BF16, name="gains")
+        nc.scalar.dma_start(out=cos_sb[:], in_=cos.rearrange("b (t p) d -> p (b t) d", p=P))
+        nc.scalar.dma_start(out=sin_sb[:], in_=sin.rearrange("b (t p) d -> p (b t) d", p=P))
+        nc.scalar.dma_start(out=gains[:, 0, :], in_=q_norm_w.partition_broadcast(P))
+        nc.scalar.dma_start(out=gains[:, 1, :], in_=k_norm_w.partition_broadcast(P))
+
+        ident = consts.tile([P, P], F32, name="ident")
+        make_identity(nc, ident[:])
+        eps_col = consts.tile([P, 1], F32, name="eps_col")
+        nc.vector.memset(eps_col[:], EPS)
+        warm = consts.tile([P, 1], F32, name="warm")
+        nc.scalar.activation(out=warm[:], in_=eps_col[:], func=ACT.Sqrt)
+
+        tables = consts.tile([P, 2, TOKEN_TILES, 2, HEAD], F32, name="tables")
+        LOW = slice(0, HEAD // 2)
+        HIGH = slice(HEAD // 2, HEAD)
+
+        def build_tables():
+            for n in range(2):
+                def gain(cols, width):
+                    return gains[:, n, cols].unsqueeze(1).to_broadcast([P, TOKEN_TILES, width])
+
+                nc.vector.tensor_tensor(
+                    out=tables[:, n, :, 0, :], in0=cos_sb[:], in1=gain(slice(0, HEAD), HEAD), op=ALU.mult
+                )
+                nc.vector.tensor_tensor(
+                    out=tables[:, n, :, 1, LOW], in0=sin_sb[:, :, HIGH], in1=gain(LOW, HEAD // 2), op=ALU.mult
+                )
+                nc.vector.scalar_tensor_tensor(
+                    out=tables[:, n, :, 1, HIGH],
+                    in0=sin_sb[:, :, LOW],
+                    scalar=-1.0,
+                    in1=gain(HIGH, HEAD // 2),
+                    op0=ALU.mult,
+                    op1=ALU.mult,
+                )
+
+        operands = {}
+
+        def new_operand(pool):
+            codes = pool.tile([P, PASSES, BLOCK], U32, align_bytes=64, name="codes")
+            scales = pool.tile([P, PASSES, BLOCK], U8, align_bytes=64, name="scales")
+            return codes, scales
+
+        def passes_of(pair):
+            return (2 * (pair % 2), 2 * (pair % 2) + 1)
+
+        def turn_pair(block, pair):
+            words = raws[block][pair // 2][:].bitcast(F32)
+            banks = []
+            for g in passes_of(pair):
+                bank = turn_psum.tile([P, 2, 2, P], F32, name="bank")
+                for u in range(2):
+                    for r in range(2):
+                        first = WORDS * r + 2 * P * g + P * u
+                        nc.tensor.transpose(bank[:, u, r, :], words[:, first : first + P], ident[:])
+                banks.append(bank)
+            return banks
+
+        def pack_pair(block, pair, banks, second_copy):
+            codes, scales = operands[block]
+            rows = slice(HALF * (pair // 2), HALF * (pair // 2 + 1))
+            grouped_pair = []
+            for bank, copy in zip(banks, (nc.scalar.copy, second_copy)):
+                grouped = group_pool.tile([P, PACK * HALF], BF16, align_bytes=64, name="grouped")
+                copy(
+                    out=grouped[:].bitcast(F32).rearrange("p (c r u) -> p c r u", r=2, u=2),
+                    in_=bank[:].rearrange("p u r c -> p c r u"),
+                )
+                grouped_pair.append(grouped)
+            for g, grouped in zip(passes_of(pair), grouped_pair):
+                nc.vector.quantize_mx(
+                    out=codes[:, g, rows].bitcast(FP8X4), scales=scales[:, g, rows], in_=grouped[:]
+                )
+
+        def project(block, t):
+            x_codes, x_scales = operands[0]
+            w_codes, w_scales = operands[block]
+            toks = slice(P * t, P * (t + 1))
+            acc = acc_psum.tile([P, BLOCK], F32, name="acc")
+            for g in range(PASSES):
+                nc.tensor.matmul_mx(
+                    out=acc[:],
+                    lhsT=x_codes[:, g, toks].bitcast(FP8X4),
+                    lhsT_scale=x_scales[:, g, toks],
+                    rhs=w_codes[:, g, :].bitcast(FP8X4),
+                    rhs_scale=w_scales[:, g, :],
+                    start=(g == 0),
+                    stop=(g == PASSES - 1),
+                )
+            return acc
+
+        def finish(block, t, acc):
+            target, n = results[block]
+            squares = small_pool.tile([P, BLOCK], BF16, name="squares")
+            sums = small_pool.tile([P, HEADS], F32, name="sums")
+            for h in range(HEADS):
+                cols = slice(HEAD * h, HEAD * (h + 1))
+                nc.scalar.activation(
+                    out=squares[:, cols], in_=acc[:, cols], func=ACT.Square, accum_out=sums[:, h : h + 1]
+                )
+            rms = small_pool.tile([P, HEADS], F32, name="rms")
+            nc.scalar.activation(out=rms[:], in_=sums[:], func=ACT.Sqrt, bias=eps_col[:], scale=1.0 / HEAD)
+            inv_rms = small_pool.tile([P, HEADS], F32, name="inv_rms")
+            nc.vector.reciprocal(out=inv_rms[:], in_=rms[:])
+            prod = prod_pool.tile([P, HEADS, 2, HEAD], F32, name="prod")
+            for h in range(HEADS):
+                nc.vector.scalar_tensor_tensor(
+                    out=prod[:, h, :, :],
+                    in0=acc[:, HEAD * h : HEAD * (h + 1)].unsqueeze(1).to_broadcast([P, 2, HEAD]),
+                    scalar=inv_rms[:, h : h + 1],
+                    in1=tables[:, n, t, :, :],
+                    op0=ALU.mult,
+                    op1=ALU.mult,
+                )
+            result = result_pool.tile([P, HEADS, HEAD], F32, name="result")
+            nc.gpsimd.tensor_tensor(
+                out=result[:, :, LOW], in0=prod[:, :, 0, LOW], in1=prod[:, :, 1, HIGH], op=ALU.add
+            )
+            nc.gpsimd.tensor_tensor(
+                out=result[:, :, HIGH], in0=prod[:, :, 0, HIGH], in1=prod[:, :, 1, LOW], op=ALU.add
+            )
+            nc.sync.dma_start(out=target[P * t : P * (t + 1), :], in_=result[:].rearrange("p h d -> p (h d)"))
+
+        operands[0] = new_operand(consts)
+        operands[1] = new_operand(weight_pool)
+        for block in range(2):
+            for pair in range(PAIRS):
+                pack_pair(block, pair, turn_pair(block, pair), nc.vector.tensor_copy)
+                if block == 0 and pair == 1:
+                    build_tables()
+
+        for block in range(1, W_BLOCKS + 1):
+            if block < W_BLOCKS:
+                operands[block + 1] = new_operand(weight_pool)
+            for t in range(TOKEN_TILES):
+                if block < W_BLOCKS:
+                    banks = turn_pair(block + 1, t)
+                acc = project(block, t)
+                if block < W_BLOCKS:
+                    pack_pair(block + 1, t, banks, nc.scalar.copy)
+                finish(block, t, acc)

@@ -50,6 +50,7 @@ def tile_qwen3nextattentionforengine_pa_kernel(
         result_pool = ctx.enter_context(tc.tile_pool(name="result", bufs=W_BLOCKS * TOKEN_TILES))
         turn_psum = ctx.enter_context(tc.psum_pool(name="turn", bufs=4))
         acc_psum = ctx.enter_context(tc.psum_pool(name="acc", bufs=4))
+        ctx.enter_context(tc.manual_schedule())
 
         raws = []
         for rows in row_blocks:

@@ -18,12 +18,8 @@ PASSES = HIDDEN // (P * PACK)
 WORDS = HIDDEN // 2
 BLOCK = 512
 HALF = BLOCK // 2
-PAIRS = 4
 HEAD = 128
-HEADS = BLOCK // HEAD
 TOKEN_TILES = 4
-Q_BLOCKS = 4
-W_BLOCKS = Q_BLOCKS + 1
 EPS = 1e-6
 
 FLOPS = 2 * 512 * (2048 + 512) * HIDDEN
@@ -37,86 +33,96 @@ def tile_qwen3nextattentionforengine_pa_kernel(
     q_flat = out_0.rearrange("b s h d -> (b s) (h d)")
     k_flat = out_1.rearrange("b s h d -> (b s) (h d)")
 
-    row_blocks = [tokens] + [Wq_query[BLOCK * b : BLOCK * (b + 1), :] for b in range(Q_BLOCKS)] + [Wk]
-    results = [None] + [(q_flat[:, BLOCK * b : BLOCK * (b + 1)], 0) for b in range(Q_BLOCKS)] + [(k_flat, 1)]
+    blocks = []
+    for first, width in ((0, HALF), (HALF, HALF), (512, BLOCK), (1024, BLOCK), (1536, BLOCK)):
+        blocks.append((Wq_query[first : first + width, :], q_flat[:, first : first + width], 0))
+    blocks.append((Wk, k_flat, 1))
+
+    halves = [("x", 0), (0, 0), ("x", 1), (1, 0)]
+    halves += [(b, h) for b in range(2, len(blocks)) for h in range(2)]
+    jobs = [(owner, h, g) for owner, h in halves for g in (0, 2)]
+    HEAD_JOBS = 4
 
     with ExitStack() as ctx:
         consts = ctx.enter_context(tc.tile_pool(name="consts", bufs=1))
-        raw_pool = ctx.enter_context(tc.tile_pool(name="raw", bufs=2 * len(row_blocks)))
+        raw_pool = ctx.enter_context(tc.tile_pool(name="raw", bufs=len(halves)))
         group_pool = ctx.enter_context(tc.tile_pool(name="grouped", bufs=6))
         weight_pool = ctx.enter_context(tc.tile_pool(name="weights", bufs=2))
         small_pool = ctx.enter_context(tc.tile_pool(name="small", bufs=4))
         prod_pool = ctx.enter_context(tc.tile_pool(name="prod", bufs=4))
-        result_pool = ctx.enter_context(tc.tile_pool(name="result", bufs=W_BLOCKS * TOKEN_TILES))
+        result_pool = ctx.enter_context(tc.tile_pool(name="result", bufs=len(blocks) * TOKEN_TILES))
         turn_psum = ctx.enter_context(tc.psum_pool(name="turn", bufs=4))
         acc_psum = ctx.enter_context(tc.psum_pool(name="acc", bufs=4))
         ctx.enter_context(tc.manual_schedule())
 
-        raws = []
-        for rows in row_blocks:
-            halves = []
-            for half in range(2):
-                raw = raw_pool.tile([P, 2 * HIDDEN], BF16, name="raw")
-                nc.sync.dma_start(
-                    out=raw[:],
-                    in_=rows[HALF * half : HALF * (half + 1), :].rearrange("(p r) k -> p (r k)", r=2),
-                )
-                halves.append(raw)
-            raws.append(halves)
+        eps_col = consts.tile([P, 1], F32, name="eps_col")
+        nc.vector.memset(eps_col[:], EPS)
+        gain_rows = consts.tile([P, 2 * HEAD], BF16, name="gain_rows")
+        nc.vector.memset(gain_rows[:], 0.0)
+        ones = consts.tile([P, P], BF16, name="ones")
+        nc.vector.memset(ones[:], 1.0)
+        ident = consts.tile([P, P], F32, name="ident")
+        make_identity(nc, ident[:])
+        warm = consts.tile([P, 1], F32, name="warm")
+        nc.scalar.activation(out=warm[:], in_=eps_col[:], func=ACT.Abs_reciprocal_sqrt)
+
+        raws = {}
+
+        def load_half(owner, h):
+            rows = tokens if owner == "x" else blocks[owner][0]
+            raw = raw_pool.tile([P, 2 * HIDDEN], BF16, name="raw")
+            nc.sync.dma_start(
+                out=raw[:], in_=rows[HALF * h : HALF * (h + 1), :].rearrange("(p r) k -> p (r k)", r=2)
+            )
+            raws[(owner, h)] = raw
 
         cos_sb = consts.tile([P, TOKEN_TILES, HEAD], BF16, name="cos_sb")
         sin_sb = consts.tile([P, TOKEN_TILES, HEAD], BF16, name="sin_sb")
-        gains = consts.tile([P, 2, HEAD], BF16, name="gains")
-        nc.scalar.dma_start(out=cos_sb[:], in_=cos.rearrange("b (t p) d -> p (b t) d", p=P))
-        nc.scalar.dma_start(out=sin_sb[:], in_=sin.rearrange("b (t p) d -> p (b t) d", p=P))
-        nc.scalar.dma_start(out=gains[:, 0, :], in_=q_norm_w.partition_broadcast(P))
-        nc.scalar.dma_start(out=gains[:, 1, :], in_=k_norm_w.partition_broadcast(P))
-
-        ident = consts.tile([P, P], F32, name="ident")
-        make_identity(nc, ident[:])
-        eps_col = consts.tile([P, 1], F32, name="eps_col")
-        nc.vector.memset(eps_col[:], EPS)
-        warm = consts.tile([P, 1], F32, name="warm")
-        nc.scalar.activation(out=warm[:], in_=eps_col[:], func=ACT.Sqrt)
+        for owner, h in halves[:2]:
+            load_half(owner, h)
+        nc.sync.dma_start(out=gain_rows[0:1, 0:HEAD], in_=q_norm_w.unsqueeze(0))
+        nc.sync.dma_start(out=gain_rows[0:1, HEAD : 2 * HEAD], in_=k_norm_w.unsqueeze(0))
+        nc.sync.dma_start(out=cos_sb[:], in_=cos.rearrange("b (t p) d -> p (b t) d", p=P))
+        nc.sync.dma_start(out=sin_sb[:], in_=sin.rearrange("b (t p) d -> p (b t) d", p=P))
+        for owner, h in halves[2:]:
+            load_half(owner, h)
 
         tables = consts.tile([P, 2, TOKEN_TILES, 2, HEAD], F32, name="tables")
         LOW = slice(0, HEAD // 2)
         HIGH = slice(HEAD // 2, HEAD)
 
         def build_tables():
+            gains = acc_psum.tile([P, 2 * HEAD], F32, name="acc")
+            nc.tensor.matmul(out=gains[:], lhsT=ones[:], rhs=gain_rows[:], start=True, stop=True)
             for n in range(2):
-                def gain(cols, width):
-                    return gains[:, n, cols].unsqueeze(1).to_broadcast([P, TOKEN_TILES, width])
-
+                gain = gains[:, HEAD * n : HEAD * (n + 1)].unsqueeze(1)
                 nc.vector.tensor_tensor(
-                    out=tables[:, n, :, 0, :], in0=cos_sb[:], in1=gain(slice(0, HEAD), HEAD), op=ALU.mult
+                    out=tables[:, n, :, 0, :],
+                    in0=cos_sb[:],
+                    in1=gain.to_broadcast([P, TOKEN_TILES, HEAD]),
+                    op=ALU.mult,
                 )
-                nc.vector.tensor_tensor(
-                    out=tables[:, n, :, 1, LOW], in0=sin_sb[:, :, HIGH], in1=gain(LOW, HEAD // 2), op=ALU.mult
-                )
-                nc.vector.scalar_tensor_tensor(
-                    out=tables[:, n, :, 1, HIGH],
-                    in0=sin_sb[:, :, LOW],
-                    scalar=-1.0,
-                    in1=gain(HIGH, HEAD // 2),
-                    op0=ALU.mult,
-                    op1=ALU.mult,
-                )
+                for here, there in ((LOW, HIGH), (HIGH, LOW)):
+                    nc.vector.tensor_tensor(
+                        out=tables[:, n, :, 1, here],
+                        in0=sin_sb[:, :, there],
+                        in1=gain[:, :, here].to_broadcast([P, TOKEN_TILES, HEAD // 2]),
+                        op=ALU.mult,
+                    )
 
         operands = {}
+        packed = set()
 
-        def new_operand(pool):
-            codes = pool.tile([P, PASSES, BLOCK], U32, align_bytes=64, name="codes")
-            scales = pool.tile([P, PASSES, BLOCK], U8, align_bytes=64, name="scales")
-            return codes, scales
-
-        def passes_of(pair):
-            return (2 * (pair % 2), 2 * (pair % 2) + 1)
-
-        def turn_pair(block, pair):
-            words = raws[block][pair // 2][:].bitcast(F32)
+        def turn(job):
+            owner, h, first_pass = job
+            if owner not in operands:
+                pool = consts if owner == "x" else weight_pool
+                codes = pool.tile([P, PASSES, BLOCK], U32, align_bytes=64, name="codes")
+                scales = pool.tile([P, PASSES, BLOCK], U8, align_bytes=64, name="scales")
+                operands[owner] = (codes, scales)
+            words = raws[(owner, h)][:].bitcast(F32)
             banks = []
-            for g in passes_of(pair):
+            for g in (first_pass, first_pass + 1):
                 bank = turn_psum.tile([P, 2, 2, P], F32, name="bank")
                 for u in range(2):
                     for r in range(2):
@@ -125,86 +131,91 @@ def tile_qwen3nextattentionforengine_pa_kernel(
                 banks.append(bank)
             return banks
 
-        def pack_pair(block, pair, banks, second_copy):
-            codes, scales = operands[block]
-            rows = slice(HALF * (pair // 2), HALF * (pair // 2 + 1))
+        def pack(job, banks):
+            owner, h, first_pass = job
+            codes, scales = operands[owner]
+            rows = slice(HALF * h, HALF * (h + 1))
             grouped_pair = []
-            for bank, copy in zip(banks, (nc.scalar.copy, second_copy)):
+            for bank in banks:
                 grouped = group_pool.tile([P, PACK * HALF], BF16, align_bytes=64, name="grouped")
-                copy(
+                nc.scalar.copy(
                     out=grouped[:].bitcast(F32).rearrange("p (c r u) -> p c r u", r=2, u=2),
                     in_=bank[:].rearrange("p u r c -> p c r u"),
                 )
                 grouped_pair.append(grouped)
-            for g, grouped in zip(passes_of(pair), grouped_pair):
+            for g, grouped in zip((first_pass, first_pass + 1), grouped_pair):
                 nc.vector.quantize_mx(
                     out=codes[:, g, rows].bitcast(FP8X4), scales=scales[:, g, rows], in_=grouped[:]
                 )
+            packed.add(job)
 
-        def project(block, t):
-            x_codes, x_scales = operands[0]
-            w_codes, w_scales = operands[block]
+        def project(b, t, width):
+            needed = [("x", t // 2, g) for g in (0, 2)]
+            needed += [(b, h, g) for h in range(width // HALF) for g in (0, 2)]
+            assert all(job in packed for job in needed)
+            x_codes, x_scales = operands["x"]
+            w_codes, w_scales = operands[b]
             toks = slice(P * t, P * (t + 1))
-            acc = acc_psum.tile([P, BLOCK], F32, name="acc")
+            acc = acc_psum.tile([P, width], F32, name="acc")
             for g in range(PASSES):
                 nc.tensor.matmul_mx(
                     out=acc[:],
                     lhsT=x_codes[:, g, toks].bitcast(FP8X4),
                     lhsT_scale=x_scales[:, g, toks],
-                    rhs=w_codes[:, g, :].bitcast(FP8X4),
-                    rhs_scale=w_scales[:, g, :],
+                    rhs=w_codes[:, g, 0:width].bitcast(FP8X4),
+                    rhs_scale=w_scales[:, g, 0:width],
                     start=(g == 0),
                     stop=(g == PASSES - 1),
                 )
             return acc
 
-        def finish(block, t, acc):
-            target, n = results[block]
-            squares = small_pool.tile([P, BLOCK], BF16, name="squares")
-            sums = small_pool.tile([P, HEADS], F32, name="sums")
-            for h in range(HEADS):
-                cols = slice(HEAD * h, HEAD * (h + 1))
+        def finish(b, t, width, acc):
+            target, n = blocks[b][1], blocks[b][2]
+            heads = width // HEAD
+            squares = small_pool.tile([P, width], BF16, name="squares")
+            sums = small_pool.tile([P, heads], F32, name="sums")
+            for hd in range(heads):
+                cols = slice(HEAD * hd, HEAD * (hd + 1))
                 nc.scalar.activation(
-                    out=squares[:, cols], in_=acc[:, cols], func=ACT.Square, accum_out=sums[:, h : h + 1]
+                    out=squares[:, cols], in_=acc[:, cols], func=ACT.Square, accum_out=sums[:, hd : hd + 1]
                 )
-            rms = small_pool.tile([P, HEADS], F32, name="rms")
-            nc.scalar.activation(out=rms[:], in_=sums[:], func=ACT.Sqrt, bias=eps_col[:], scale=1.0 / HEAD)
-            inv_rms = small_pool.tile([P, HEADS], F32, name="inv_rms")
-            nc.vector.reciprocal(out=inv_rms[:], in_=rms[:])
-            prod = prod_pool.tile([P, HEADS, 2, HEAD], F32, name="prod")
-            for h in range(HEADS):
+            inv_rms = small_pool.tile([P, heads], F32, name="inv_rms")
+            nc.scalar.activation(
+                out=inv_rms[:], in_=sums[:], func=ACT.Abs_reciprocal_sqrt, bias=eps_col[:], scale=1.0 / HEAD
+            )
+            prod = prod_pool.tile([P, heads, 2, HEAD], F32, name="prod")
+            for hd in range(heads):
                 nc.vector.scalar_tensor_tensor(
-                    out=prod[:, h, :, :],
-                    in0=acc[:, HEAD * h : HEAD * (h + 1)].unsqueeze(1).to_broadcast([P, 2, HEAD]),
-                    scalar=inv_rms[:, h : h + 1],
+                    out=prod[:, hd, :, :],
+                    in0=acc[:, HEAD * hd : HEAD * (hd + 1)].unsqueeze(1).to_broadcast([P, 2, HEAD]),
+                    scalar=inv_rms[:, hd : hd + 1],
                     in1=tables[:, n, t, :, :],
                     op0=ALU.mult,
                     op1=ALU.mult,
                 )
-            result = result_pool.tile([P, HEADS, HEAD], F32, name="result")
+            result = result_pool.tile([P, heads, HEAD], F32, name="result")
             nc.gpsimd.tensor_tensor(
-                out=result[:, :, LOW], in0=prod[:, :, 0, LOW], in1=prod[:, :, 1, HIGH], op=ALU.add
+                out=result[:, :, LOW], in0=prod[:, :, 0, LOW], in1=prod[:, :, 1, HIGH], op=ALU.subtract
             )
             nc.gpsimd.tensor_tensor(
                 out=result[:, :, HIGH], in0=prod[:, :, 0, HIGH], in1=prod[:, :, 1, LOW], op=ALU.add
             )
             nc.sync.dma_start(out=target[P * t : P * (t + 1), :], in_=result[:].rearrange("p h d -> p (h d)"))
 
-        operands[0] = new_operand(consts)
-        operands[1] = new_operand(weight_pool)
-        for block in range(2):
-            for pair in range(PAIRS):
-                pack_pair(block, pair, turn_pair(block, pair), nc.vector.tensor_copy)
-                if block == 0 and pair == 1:
-                    build_tables()
+        for job in jobs[:HEAD_JOBS]:
+            pack(job, turn(job))
+        build_tables()
 
-        for block in range(1, W_BLOCKS + 1):
-            if block < W_BLOCKS:
-                operands[block + 1] = new_operand(weight_pool)
+        later_jobs = jobs[HEAD_JOBS:]
+        step = 0
+        for b in range(len(blocks)):
+            width = blocks[b][0].shape[0]
             for t in range(TOKEN_TILES):
-                if block < W_BLOCKS:
-                    banks = turn_pair(block + 1, t)
-                acc = project(block, t)
-                if block < W_BLOCKS:
-                    pack_pair(block + 1, t, banks, nc.scalar.copy)
-                finish(block, t, acc)
+                job = later_jobs[step] if step < len(later_jobs) else None
+                if job is not None:
+                    banks = turn(job)
+                acc = project(b, t, width)
+                if job is not None:
+                    pack(job, banks)
+                finish(b, t, width, acc)
+                step += 1

@@ -21,6 +21,7 @@ HALF = BLOCK // 2
 HEAD = 128
 TOKEN_TILES = 4
 EPS = 1e-6
+STEPS_PER_TURN = 2
 
 FLOPS = 2 * 512 * (2048 + 512) * HIDDEN
 
@@ -78,13 +79,13 @@ def tile_qwen3nextattentionforengine_pa_kernel(
 
         cos_sb = consts.tile([P, TOKEN_TILES, HEAD], BF16, name="cos_sb")
         sin_sb = consts.tile([P, TOKEN_TILES, HEAD], BF16, name="sin_sb")
-        for owner, h in halves[:2]:
+        for owner, h in halves[:3]:
             load_half(owner, h)
         nc.sync.dma_start(out=gain_rows[0:1, 0:HEAD], in_=q_norm_w.unsqueeze(0))
         nc.sync.dma_start(out=gain_rows[0:1, HEAD : 2 * HEAD], in_=k_norm_w.unsqueeze(0))
         nc.sync.dma_start(out=cos_sb[:], in_=cos.rearrange("b (t p) d -> p (b t) d", p=P))
         nc.sync.dma_start(out=sin_sb[:], in_=sin.rearrange("b (t p) d -> p (b t) d", p=P))
-        for owner, h in halves[2:]:
+        for owner, h in halves[3:]:
             load_half(owner, h)
 
         tables = consts.tile([P, 2, TOKEN_TILES, 2, HEAD], F32, name="tables")
@@ -102,12 +103,14 @@ def tile_qwen3nextattentionforengine_pa_kernel(
                     in1=gain.to_broadcast([P, TOKEN_TILES, HEAD]),
                     op=ALU.mult,
                 )
-                for here, there in ((LOW, HIGH), (HIGH, LOW)):
-                    nc.vector.tensor_tensor(
+                for here, there, sign in ((LOW, HIGH, 1.0), (HIGH, LOW, -1.0)):
+                    nc.vector.scalar_tensor_tensor(
                         out=tables[:, n, :, 1, here],
                         in0=sin_sb[:, :, there],
+                        scalar=sign,
                         in1=gain[:, :, here].to_broadcast([P, TOKEN_TILES, HEAD // 2]),
-                        op=ALU.mult,
+                        op0=ALU.mult,
+                        op1=ALU.mult,
                     )
 
         operands = {}
@@ -149,7 +152,8 @@ def tile_qwen3nextattentionforengine_pa_kernel(
                 )
             packed.add(job)
 
-        def project(b, t, width):
+        def project(b, t):
+            width = blocks[b][0].shape[0]
             needed = [("x", t // 2, g) for g in (0, 2)]
             needed += [(b, h, g) for h in range(width // HALF) for g in (0, 2)]
             assert all(job in packed for job in needed)
@@ -169,8 +173,9 @@ def tile_qwen3nextattentionforengine_pa_kernel(
                 )
             return acc
 
-        def finish(b, t, width, acc):
-            target, n = blocks[b][1], blocks[b][2]
+        def finish(b, t, acc):
+            rows, target, n = blocks[b]
+            width = rows.shape[0]
             heads = width // HEAD
             squares = small_pool.tile([P, width], BF16, name="squares")
             sums = small_pool.tile([P, heads], F32, name="sums")
@@ -193,29 +198,24 @@ def tile_qwen3nextattentionforengine_pa_kernel(
                     op0=ALU.mult,
                     op1=ALU.mult,
                 )
-            result = result_pool.tile([P, heads, HEAD], F32, name="result")
-            nc.gpsimd.tensor_tensor(
-                out=result[:, :, LOW], in0=prod[:, :, 0, LOW], in1=prod[:, :, 1, HIGH], op=ALU.subtract
-            )
-            nc.gpsimd.tensor_tensor(
-                out=result[:, :, HIGH], in0=prod[:, :, 0, HIGH], in1=prod[:, :, 1, LOW], op=ALU.add
-            )
-            nc.sync.dma_start(out=target[P * t : P * (t + 1), :], in_=result[:].rearrange("p h d -> p (h d)"))
+            result = result_pool.tile([P, heads, 2, HEAD // 2], F32, name="result")
+            stay = prod[:, :, 0, :].rearrange("p h (s d) -> p h s d", s=2)
+            cross = prod[:, :, 1, :].rearrange("p h (s d) -> p h s d", s=2)
+            nc.gpsimd.tensor_tensor(out=result[:], in0=stay, in1=cross[:, :, ::-1, :], op=ALU.add)
+            nc.sync.dma_start(out=target[P * t : P * (t + 1), :], in_=result[:].rearrange("p h s d -> p (h s d)"))
 
         for job in jobs[:HEAD_JOBS]:
             pack(job, turn(job))
         build_tables()
 
         later_jobs = jobs[HEAD_JOBS:]
-        step = 0
-        for b in range(len(blocks)):
-            width = blocks[b][0].shape[0]
-            for t in range(TOKEN_TILES):
-                job = later_jobs[step] if step < len(later_jobs) else None
-                if job is not None:
-                    banks = turn(job)
-                acc = project(b, t, width)
-                if job is not None:
-                    pack(job, banks)
-                finish(b, t, width, acc)
-                step += 1
+        steps = [(b, t) for b in range(len(blocks)) for t in range(TOKEN_TILES)]
+        for first in range(0, len(steps), STEPS_PER_TURN):
+            turn_steps = steps[first : first + STEPS_PER_TURN]
+            turn_jobs = later_jobs[first : first + STEPS_PER_TURN]
+            turned = [turn(job) for job in turn_jobs]
+            accs = [project(b, t) for b, t in turn_steps]
+            for job, banks in zip(turn_jobs, turned):
+                pack(job, banks)
+            for (b, t), acc in zip(turn_steps, accs):
+                finish(b, t, acc)

@@ -21,7 +21,7 @@ HALF = BLOCK // 2
 HEAD = 128
 TOKEN_TILES = 4
 EPS = 1e-6
-STEPS_PER_TURN = 2
+STEPS_PER_TURN = 1
 
 FLOPS = 2 * 512 * (2048 + 512) * HIDDEN
 

from contextlib import ExitStack

import concourse.mybir as mybir
from concourse.masks import make_identity

F32 = mybir.dt.float32
BF16 = mybir.dt.bfloat16
U32 = mybir.dt.uint32
U8 = mybir.dt.uint8
FP8X4 = mybir.dt.float8_e4m3fn_x4
ACT = mybir.ActivationFunctionType
ALU = mybir.AluOpType

P = 128
PACK = 4
HIDDEN = 2048
PASSES = HIDDEN // (P * PACK)
WORDS = HIDDEN // 2
BLOCK = 512
HALF = BLOCK // 2
HEAD = 128
TOKEN_TILES = 4
EPS = 1e-6
STEPS_PER_TURN = 1

FLOPS = 2 * 512 * (2048 + 512) * HIDDEN


def tile_qwen3nextattentionforengine_pa_kernel(
    tc, hidden_states, cos, sin, Wq_query, Wk, q_norm_w, k_norm_w, out_0, out_1
):
    nc = tc.nc
    tokens = hidden_states.rearrange("b s k -> (b s) k")
    q_flat = out_0.rearrange("b s h d -> (b s) (h d)")
    k_flat = out_1.rearrange("b s h d -> (b s) (h d)")

    blocks = []
    for first, width in ((0, HALF), (HALF, HALF), (512, BLOCK), (1024, BLOCK), (1536, BLOCK)):
        blocks.append((Wq_query[first : first + width, :], q_flat[:, first : first + width], 0))
    blocks.append((Wk, k_flat, 1))

    halves = [("x", 0), (0, 0), ("x", 1), (1, 0)]
    halves += [(b, h) for b in range(2, len(blocks)) for h in range(2)]
    jobs = [(owner, h, g) for owner, h in halves for g in (0, 2)]
    HEAD_JOBS = 4

    with ExitStack() as ctx:
        consts = ctx.enter_context(tc.tile_pool(name="consts", bufs=1))
        raw_pool = ctx.enter_context(tc.tile_pool(name="raw", bufs=len(halves)))
        group_pool = ctx.enter_context(tc.tile_pool(name="grouped", bufs=6))
        weight_pool = ctx.enter_context(tc.tile_pool(name="weights", bufs=2))
        small_pool = ctx.enter_context(tc.tile_pool(name="small", bufs=4))
        prod_pool = ctx.enter_context(tc.tile_pool(name="prod", bufs=4))
        result_pool = ctx.enter_context(tc.tile_pool(name="result", bufs=len(blocks) * TOKEN_TILES))
        turn_psum = ctx.enter_context(tc.psum_pool(name="turn", bufs=4))
        acc_psum = ctx.enter_context(tc.psum_pool(name="acc", bufs=4))
        ctx.enter_context(tc.manual_schedule())

        eps_col = consts.tile([P, 1], F32, name="eps_col")
        nc.vector.memset(eps_col[:], EPS)
        gain_rows = consts.tile([P, 2 * HEAD], BF16, name="gain_rows")
        nc.vector.memset(gain_rows[:], 0.0)
        ones = consts.tile([P, P], BF16, name="ones")
        nc.vector.memset(ones[:], 1.0)
        ident = consts.tile([P, P], F32, name="ident")
        make_identity(nc, ident[:])
        warm = consts.tile([P, 1], F32, name="warm")
        nc.scalar.activation(out=warm[:], in_=eps_col[:], func=ACT.Abs_reciprocal_sqrt)

        raws = {}

        def load_half(owner, h):
            rows = tokens if owner == "x" else blocks[owner][0]
            raw = raw_pool.tile([P, 2 * HIDDEN], BF16, name="raw")
            nc.sync.dma_start(
                out=raw[:], in_=rows[HALF * h : HALF * (h + 1), :].rearrange("(p r) k -> p (r k)", r=2)
            )
            raws[(owner, h)] = raw

        cos_sb = consts.tile([P, TOKEN_TILES, HEAD], BF16, name="cos_sb")
        sin_sb = consts.tile([P, TOKEN_TILES, HEAD], BF16, name="sin_sb")
        for owner, h in halves[:3]:
            load_half(owner, h)
        nc.sync.dma_start(out=gain_rows[0:1, 0:HEAD], in_=q_norm_w.unsqueeze(0))
        nc.sync.dma_start(out=gain_rows[0:1, HEAD : 2 * HEAD], in_=k_norm_w.unsqueeze(0))
        nc.sync.dma_start(out=cos_sb[:], in_=cos.rearrange("b (t p) d -> p (b t) d", p=P))
        nc.sync.dma_start(out=sin_sb[:], in_=sin.rearrange("b (t p) d -> p (b t) d", p=P))
        for owner, h in halves[3:]:
            load_half(owner, h)

        tables = consts.tile([P, 2, TOKEN_TILES, 2, HEAD], F32, name="tables")
        LOW = slice(0, HEAD // 2)
        HIGH = slice(HEAD // 2, HEAD)

        def build_tables():
            gains = acc_psum.tile([P, 2 * HEAD], F32, name="acc")
            nc.tensor.matmul(out=gains[:], lhsT=ones[:], rhs=gain_rows[:], start=True, stop=True)
            for n in range(2):
                gain = gains[:, HEAD * n : HEAD * (n + 1)].unsqueeze(1)
                nc.vector.tensor_tensor(
                    out=tables[:, n, :, 0, :],
                    in0=cos_sb[:],
                    in1=gain.to_broadcast([P, TOKEN_TILES, HEAD]),
                    op=ALU.mult,
                )
                for here, there, sign in ((LOW, HIGH, 1.0), (HIGH, LOW, -1.0)):
                    nc.vector.scalar_tensor_tensor(
                        out=tables[:, n, :, 1, here],
                        in0=sin_sb[:, :, there],
                        scalar=sign,
                        in1=gain[:, :, here].to_broadcast([P, TOKEN_TILES, HEAD // 2]),
                        op0=ALU.mult,
                        op1=ALU.mult,
                    )

        operands = {}
        packed = set()

        def turn(job):
            owner, h, first_pass = job
            if owner not in operands:
                pool = consts if owner == "x" else weight_pool
                codes = pool.tile([P, PASSES, BLOCK], U32, align_bytes=64, name="codes")
                scales = pool.tile([P, PASSES, BLOCK], U8, align_bytes=64, name="scales")
                operands[owner] = (codes, scales)
            words = raws[(owner, h)][:].bitcast(F32)
            banks = []
            for g in (first_pass, first_pass + 1):
                bank = turn_psum.tile([P, 2, 2, P], F32, name="bank")
                for u in range(2):
                    for r in range(2):
                        first = WORDS * r + 2 * P * g + P * u
                        nc.tensor.transpose(bank[:, u, r, :], words[:, first : first + P], ident[:])
                banks.append(bank)
            return banks

        def pack(job, banks):
            owner, h, first_pass = job
            codes, scales = operands[owner]
            rows = slice(HALF * h, HALF * (h + 1))
            grouped_pair = []
            for bank in banks:
                grouped = group_pool.tile([P, PACK * HALF], BF16, align_bytes=64, name="grouped")
                nc.scalar.copy(
                    out=grouped[:].bitcast(F32).rearrange("p (c r u) -> p c r u", r=2, u=2),
                    in_=bank[:].rearrange("p u r c -> p c r u"),
                )
                grouped_pair.append(grouped)
            for g, grouped in zip((first_pass, first_pass + 1), grouped_pair):
                nc.vector.quantize_mx(
                    out=codes[:, g, rows].bitcast(FP8X4), scales=scales[:, g, rows], in_=grouped[:]
                )
            packed.add(job)

        def project(b, t):
            width = blocks[b][0].shape[0]
            needed = [("x", t // 2, g) for g in (0, 2)]
            needed += [(b, h, g) for h in range(width // HALF) for g in (0, 2)]
            assert all(job in packed for job in needed)
            x_codes, x_scales = operands["x"]
            w_codes, w_scales = operands[b]
            toks = slice(P * t, P * (t + 1))
            acc = acc_psum.tile([P, width], F32, name="acc")
            for g in range(PASSES):
                nc.tensor.matmul_mx(
                    out=acc[:],
                    lhsT=x_codes[:, g, toks].bitcast(FP8X4),
                    lhsT_scale=x_scales[:, g, toks],
                    rhs=w_codes[:, g, 0:width].bitcast(FP8X4),
                    rhs_scale=w_scales[:, g, 0:width],
                    start=(g == 0),
                    stop=(g == PASSES - 1),
                )
            return acc

        def finish(b, t, acc):
            rows, target, n = blocks[b]
            width = rows.shape[0]
            heads = width // HEAD
            squares = small_pool.tile([P, width], BF16, name="squares")
            sums = small_pool.tile([P, heads], F32, name="sums")
            for hd in range(heads):
                cols = slice(HEAD * hd, HEAD * (hd + 1))
                nc.scalar.activation(
                    out=squares[:, cols], in_=acc[:, cols], func=ACT.Square, accum_out=sums[:, hd : hd + 1]
                )
            inv_rms = small_pool.tile([P, heads], F32, name="inv_rms")
            nc.scalar.activation(
                out=inv_rms[:], in_=sums[:], func=ACT.Abs_reciprocal_sqrt, bias=eps_col[:], scale=1.0 / HEAD
            )
            prod = prod_pool.tile([P, heads, 2, HEAD], F32, name="prod")
            for hd in range(heads):
                nc.vector.scalar_tensor_tensor(
                    out=prod[:, hd, :, :],
                    in0=acc[:, HEAD * hd : HEAD * (hd + 1)].unsqueeze(1).to_broadcast([P, 2, HEAD]),
                    scalar=inv_rms[:, hd : hd + 1],
                    in1=tables[:, n, t, :, :],
                    op0=ALU.mult,
                    op1=ALU.mult,
                )
            result = result_pool.tile([P, heads, 2, HEAD // 2], F32, name="result")
            stay = prod[:, :, 0, :].rearrange("p h (s d) -> p h s d", s=2)
            cross = prod[:, :, 1, :].rearrange("p h (s d) -> p h s d", s=2)
            nc.gpsimd.tensor_tensor(out=result[:], in0=stay, in1=cross[:, :, ::-1, :], op=ALU.add)
            nc.sync.dma_start(out=target[P * t : P * (t + 1), :], in_=result[:].rearrange("p h s d -> p (h s d)"))

        for job in jobs[:HEAD_JOBS]:
            pack(job, turn(job))
        build_tables()

        later_jobs = jobs[HEAD_JOBS:]
        steps = [(b, t) for b in range(len(blocks)) for t in range(TOKEN_TILES)]
        for first in range(0, len(steps), STEPS_PER_TURN):
            turn_steps = steps[first : first + STEPS_PER_TURN]
            turn_jobs = later_jobs[first : first + STEPS_PER_TURN]
            turned = [turn(job) for job in turn_jobs]
            accs = [project(b, t) for b, t in turn_steps]
            for job, banks in zip(turn_jobs, turned):
                pack(job, banks)
            for (b, t), acc in zip(turn_steps, accs):
                finish(b, t, acc)
